import numpy as np
import ml_dtypes

BF16 = ml_dtypes.bfloat16


def bf(x):
    return np.asarray(x, np.float32).astype(BF16)


def f32(x):
    return np.asarray(x, np.float32)


def f64(x):
    return np.asarray(x).astype(np.float64)


def striped(idx):
    return np.tile(idx.reshape(-1, 16).T, (8, 1))


D, E, H, S, N = 128, 128, 512, 512, 1024


def sigmoid(v):
    return 1.0 / (1.0 + np.exp(-v))


def setup_inputs():
    return {"table": bf(np.random.standard_normal((E, S))), "w": bf(np.random.standard_normal((E, D)) / np.sqrt(E)), "b": f32(np.random.standard_normal((D, 1)) / np.sqrt(E)), "q": bf(np.random.standard_normal((D, N))), "p": f32(np.random.standard_normal((D, N))), "vw1": bf(np.random.standard_normal((H, D)) / np.sqrt(D)), "vb1": f32(0.5 * np.random.standard_normal((H, 1))), "vw2": f32(np.random.standard_normal((H, 1)) * np.sqrt(D / H)), "offs": striped(np.random.permutation(np.tile(np.arange(S), 2))[:N])}


def reference(table, w, b, q, p, vw1, vb1, vw2, offs):
    idx = offs[:16].T.reshape(-1)
    force = f64(w).T @ f64(table)[:, idx] + f64(b)
    h = f64(vw1) @ f64(q) + f64(vb1)
    s = sigmoid(h) * f64(vw2)
    grad = f64(vw1).T @ s
    return f64(p) - grad + force

@@ -1,0 +1,79 @@
+import concourse.mybir as mybir
+from concourse.masks import make_identity
+
+BF16 = mybir.dt.bfloat16
+F32 = mybir.dt.float32
+U16 = mybir.dt.uint16
+MULT = mybir.AluOpType.mult
+ADD = mybir.AluOpType.add
+SIGMOID = mybir.ActivationFunctionType.Sigmoid
+
+P = 128
+H = 512
+S = 512
+N = 1024
+PIECE = 512
+N_PIECES = N // PIECE
+N_BLOCKS = H // P
+FLOPS = 2 * P * P * N + 2 * 2 * H * P * N
+
+
+def tile_latenthamiltonianpredictor_kernel(tc, table, w, b, q, p, vw1, vb1, vw2, offs, out):
+    nc = tc.nc
+    with (
+        tc.tile_pool(name="held", bufs=1) as held,
+        tc.tile_pool(name="work", bufs=3) as work,
+        tc.psum_pool(name="flip", bufs=1) as flip,
+        tc.psum_pool(name="hidden", bufs=4) as hidden,
+        tc.psum_pool(name="kicks", bufs=1) as kicks,
+    ):
+        vw1_sb = held.tile([P, H], BF16)
+        nc.sync.dma_start(vw1_sb[:], vw1.rearrange("(r kb) i -> r (kb i)", kb=N_BLOCKS))
+        q_sb = [held.tile([P, PIECE], BF16, name=f"q_sb{c}") for c in range(N_PIECES)]
+        for c in range(N_PIECES):
+            nc.sync.dma_start(q_sb[c][:], q[:, c * PIECE : (c + 1) * PIECE])
+        offsets = held.tile([P, N // 16], U16)
+        nc.sync.dma_start(offsets[:], offs)
+
+        vb1_sb = held.tile([P, N_BLOCKS], F32)
+        nc.scalar.dma_start(vb1_sb[:], vb1.rearrange("(r kb) one -> r (kb one)", kb=N_BLOCKS))
+        vw2_sb = held.tile([P, N_BLOCKS], F32)
+        nc.scalar.dma_start(vw2_sb[:], vw2.rearrange("(r kb) one -> r (kb one)", kb=N_BLOCKS))
+        table_sb = held.tile([P, S], BF16)
+        nc.scalar.dma_start(table_sb[:], table)
+        w_sb = held.tile([P, P], BF16)
+        nc.scalar.dma_start(w_sb[:], w)
+        b_sb = held.tile([P, 1], F32)
+        nc.scalar.dma_start(b_sb[:], b)
+
+        identity = held.tile([P, P], BF16)
+        make_identity(nc, identity[:])
+        p_sb = [held.tile([P, PIECE], F32, name=f"p_sb{c}") for c in range(N_PIECES)]
+        for c in range(N_PIECES):
+            nc.gpsimd.dma_start(p_sb[c][:], p[:, c * PIECE : (c + 1) * PIECE])
+
+        vw1T_ps = flip.tile([P, H], BF16)
+        for kb in range(N_BLOCKS):
+            block = slice(kb * P, (kb + 1) * P)
+            nc.tensor.transpose(vw1T_ps[:, block], vw1_sb[:, block], identity[:])
+        vw1T_sb = held.tile([P, H], BF16)
+        nc.vector.tensor_copy(vw1T_sb[:], vw1T_ps[:])
+
+        kick = [kicks.tile([P, PIECE], F32, name=f"kick{c}") for c in range(N_PIECES)]
+        for c in range(N_PIECES):
+            piece_offsets = offsets[:, c * (PIECE // 16) : (c + 1) * (PIECE // 16)]
+            nc.tensor.matmul(kick[c][:], w_sb[:], table_sb[:].indirect(piece_offsets), start=True, stop=False)
+
+        for c in range(N_PIECES):
+            for kb in range(N_BLOCKS):
+                block = slice(kb * P, (kb + 1) * P)
+                h = hidden.tile([P, PIECE], F32)
+                nc.tensor.matmul(h[:], vw1T_sb[:, block], q_sb[c][:], start=True, stop=True)
+                sig = work.tile([P, PIECE], F32)
+                nc.scalar.activation(sig[:], h[:], SIGMOID, bias=vb1_sb[:, kb : kb + 1])
+                minus_s = work.tile([P, PIECE], BF16)
+                nc.vector.tensor_scalar(minus_s[:], sig[:], vw2_sb[:, kb : kb + 1], -1.0, MULT, MULT)
+                nc.tensor.matmul(kick[c][:], vw1_sb[:, block], minus_s[:], start=False, stop=(kb == N_BLOCKS - 1))
+            result = work.tile([P, PIECE], F32)
+            nc.vector.scalar_tensor_tensor(result[:], kick[c][:], b_sb[:, 0:1], p_sb[c][:], ADD, ADD)
+            nc.sync.dma_start(out[:, c * PIECE : (c + 1) * PIECE], result[:])

@@ -15,6 +15,8 @@ N = 1024
 PIECE = 512
 N_PIECES = N // PIECE
 N_BLOCKS = H // P
+N_CHUNKS = N_PIECES * N_BLOCKS
+AHEAD = 4
 FLOPS = 2 * P * P * N + 2 * 2 * H * P * N
 
 
@@ -24,34 +26,32 @@ def tile_latenthamiltonianpredictor_kernel(tc, table, w, b, q, p, vw1, vb1, vw2,
         tc.tile_pool(name="held", bufs=1) as held,
         tc.tile_pool(name="work", bufs=3) as work,
         tc.psum_pool(name="flip", bufs=1) as flip,
-        tc.psum_pool(name="hidden", bufs=4) as hidden,
+        tc.psum_pool(name="hidden", bufs=AHEAD) as hidden,
         tc.psum_pool(name="kicks", bufs=1) as kicks,
     ):
         vw1_sb = held.tile([P, H], BF16)
-        nc.sync.dma_start(vw1_sb[:], vw1.rearrange("(r kb) i -> r (kb i)", kb=N_BLOCKS))
-        q_sb = [held.tile([P, PIECE], BF16, name=f"q_sb{c}") for c in range(N_PIECES)]
-        for c in range(N_PIECES):
-            nc.sync.dma_start(q_sb[c][:], q[:, c * PIECE : (c + 1) * PIECE])
-        offsets = held.tile([P, N // 16], U16)
-        nc.sync.dma_start(offsets[:], offs)
-
         vb1_sb = held.tile([P, N_BLOCKS], F32)
-        nc.scalar.dma_start(vb1_sb[:], vb1.rearrange("(r kb) one -> r (kb one)", kb=N_BLOCKS))
         vw2_sb = held.tile([P, N_BLOCKS], F32)
-        nc.scalar.dma_start(vw2_sb[:], vw2.rearrange("(r kb) one -> r (kb one)", kb=N_BLOCKS))
-        table_sb = held.tile([P, S], BF16)
-        nc.scalar.dma_start(table_sb[:], table)
+        offsets = held.tile([P, N // 16], U16)
         w_sb = held.tile([P, P], BF16)
-        nc.scalar.dma_start(w_sb[:], w)
+        table_sb = held.tile([P, S], BF16)
         b_sb = held.tile([P, 1], F32)
+        q_sb = [held.tile([P, PIECE], BF16, name=f"q_sb{c}") for c in range(N_PIECES)]
+        p_sb = [held.tile([P, PIECE], F32, name=f"p_sb{c}") for c in range(N_PIECES)]
+        nc.sync.dma_start(vw1_sb[:], vw1.rearrange("(r kb) i -> r (kb i)", kb=N_BLOCKS))
+        nc.scalar.dma_start(q_sb[0][:], q[:, 0:PIECE])
+        nc.sync.dma_start(vb1_sb[:], vb1.rearrange("(r kb) one -> r (kb one)", kb=N_BLOCKS))
+        nc.scalar.dma_start(q_sb[1][:], q[:, PIECE:N])
+        nc.sync.dma_start(vw2_sb[:], vw2.rearrange("(r kb) one -> r (kb one)", kb=N_BLOCKS))
+        nc.scalar.dma_start(table_sb[:], table)
+        nc.sync.dma_start(offsets[:], offs)
+        nc.sync.dma_start(w_sb[:], w)
         nc.scalar.dma_start(b_sb[:], b)
+        nc.sync.dma_start(p_sb[0][:], p[:, 0:PIECE])
+        nc.scalar.dma_start(p_sb[1][:], p[:, PIECE:N])
 
         identity = held.tile([P, P], BF16)
         make_identity(nc, identity[:])
-        p_sb = [held.tile([P, PIECE], F32, name=f"p_sb{c}") for c in range(N_PIECES)]
-        for c in range(N_PIECES):
-            nc.gpsimd.dma_start(p_sb[c][:], p[:, c * PIECE : (c + 1) * PIECE])
-
         vw1T_ps = flip.tile([P, H], BF16)
         for kb in range(N_BLOCKS):
             block = slice(kb * P, (kb + 1) * P)
@@ -59,21 +59,32 @@ def tile_latenthamiltonianpredictor_kernel(tc, table, w, b, q, p, vw1, vb1, vw2,
         vw1T_sb = held.tile([P, H], BF16)
         nc.vector.tensor_copy(vw1T_sb[:], vw1T_ps[:])
 
+        h = {}
+
+        def hidden_layer(chunk):
+            c, kb = divmod(chunk, N_BLOCKS)
+            h[chunk] = hidden.tile([P, PIECE], F32, name="h")
+            nc.tensor.matmul(h[chunk][:], vw1T_sb[:, kb * P : (kb + 1) * P], q_sb[c][:], start=True, stop=True)
+
+        for chunk in range(AHEAD):
+            hidden_layer(chunk)
+
         kick = [kicks.tile([P, PIECE], F32, name=f"kick{c}") for c in range(N_PIECES)]
         for c in range(N_PIECES):
             piece_offsets = offsets[:, c * (PIECE // 16) : (c + 1) * (PIECE // 16)]
             nc.tensor.matmul(kick[c][:], w_sb[:], table_sb[:].indirect(piece_offsets), start=True, stop=False)
 
-        for c in range(N_PIECES):
-            for kb in range(N_BLOCKS):
-                block = slice(kb * P, (kb + 1) * P)
-                h = hidden.tile([P, PIECE], F32)
-                nc.tensor.matmul(h[:], vw1T_sb[:, block], q_sb[c][:], start=True, stop=True)
-                sig = work.tile([P, PIECE], F32)
-                nc.scalar.activation(sig[:], h[:], SIGMOID, bias=vb1_sb[:, kb : kb + 1])
-                minus_s = work.tile([P, PIECE], BF16)
-                nc.vector.tensor_scalar(minus_s[:], sig[:], vw2_sb[:, kb : kb + 1], -1.0, MULT, MULT)
-                nc.tensor.matmul(kick[c][:], vw1_sb[:, block], minus_s[:], start=False, stop=(kb == N_BLOCKS - 1))
-            result = work.tile([P, PIECE], F32)
-            nc.vector.scalar_tensor_tensor(result[:], kick[c][:], b_sb[:, 0:1], p_sb[c][:], ADD, ADD)
-            nc.sync.dma_start(out[:, c * PIECE : (c + 1) * PIECE], result[:])
+        for chunk in range(N_CHUNKS):
+            c, kb = divmod(chunk, N_BLOCKS)
+            sig = work.tile([P, PIECE], F32)
+            nc.scalar.activation(sig[:], h[chunk][:], SIGMOID, bias=vb1_sb[:, kb : kb + 1])
+            if chunk + AHEAD < N_CHUNKS:
+                hidden_layer(chunk + AHEAD)
+            minus_s = work.tile([P, PIECE], BF16)
+            nc.vector.tensor_scalar(minus_s[:], sig[:], vw2_sb[:, kb : kb + 1], -1.0, MULT, MULT)
+            last_block = kb == N_BLOCKS - 1
+            nc.tensor.matmul(kick[c][:], vw1_sb[:, kb * P : (kb + 1) * P], minus_s[:], start=False, stop=last_block)
+            if last_block:
+                result = work.tile([P, PIECE], F32)
+                nc.vector.scalar_tensor_tensor(result[:], kick[c][:], b_sb[:, 0:1], p_sb[c][:], ADD, ADD)
+                nc.sync.dma_start(out[:, c * PIECE : (c + 1) * PIECE], result[:])

@@ -17,6 +17,7 @@ N_PIECES = N // PIECE
 N_BLOCKS = H // P
 N_CHUNKS = N_PIECES * N_BLOCKS
 AHEAD = 4
+WARM_UP = 8
 FLOPS = 2 * P * P * N + 2 * 2 * H * P * N
 
 
@@ -25,10 +26,16 @@ def tile_latenthamiltonianpredictor_kernel(tc, table, w, b, q, p, vw1, vb1, vw2,
     with (
         tc.tile_pool(name="held", bufs=1) as held,
         tc.tile_pool(name="work", bufs=3) as work,
-        tc.psum_pool(name="flip", bufs=1) as flip,
+        tc.psum_pool(name="flip", bufs=2) as flip,
         tc.psum_pool(name="hidden", bufs=AHEAD) as hidden,
         tc.psum_pool(name="kicks", bufs=1) as kicks,
     ):
+        zeros = held.tile([P, PIECE], BF16)
+        nc.vector.memset(zeros[:], 0.0)
+        warm = hidden.tile([P, PIECE], F32, tag="h")
+        for turn in range(WARM_UP):
+            nc.tensor.matmul(warm[:], zeros[:, 0:P], zeros[:], start=True, stop=True)
+
         vw1_sb = held.tile([P, H], BF16)
         vb1_sb = held.tile([P, N_BLOCKS], F32)
         vw2_sb = held.tile([P, N_BLOCKS], F32)
@@ -47,23 +54,23 @@ def tile_latenthamiltonianpredictor_kernel(tc, table, w, b, q, p, vw1, vb1, vw2,
         nc.sync.dma_start(offsets[:], offs)
         nc.sync.dma_start(w_sb[:], w)
         nc.scalar.dma_start(b_sb[:], b)
-        nc.sync.dma_start(p_sb[0][:], p[:, 0:PIECE])
-        nc.scalar.dma_start(p_sb[1][:], p[:, PIECE:N])
 
         identity = held.tile([P, P], BF16)
         make_identity(nc, identity[:])
-        vw1T_ps = flip.tile([P, H], BF16)
+        vw1T_sb = held.tile([P, H], BF16)
         for kb in range(N_BLOCKS):
             block = slice(kb * P, (kb + 1) * P)
-            nc.tensor.transpose(vw1T_ps[:, block], vw1_sb[:, block], identity[:])
-        vw1T_sb = held.tile([P, H], BF16)
-        nc.vector.tensor_copy(vw1T_sb[:], vw1T_ps[:])
+            vw1T_ps = flip.tile([P, P], BF16)
+            nc.tensor.transpose(vw1T_ps[:], vw1_sb[:, block], identity[:])
+            nc.vector.tensor_copy(vw1T_sb[:, block], vw1T_ps[:])
+        for c in range(N_PIECES):
+            nc.gpsimd.dma_start(p_sb[c][:], p[:, c * PIECE : (c + 1) * PIECE])
 
         h = {}
 
         def hidden_layer(chunk):
             c, kb = divmod(chunk, N_BLOCKS)
-            h[chunk] = hidden.tile([P, PIECE], F32, name="h")
+            h[chunk] = hidden.tile([P, PIECE], F32, name="h", tag="h")
             nc.tensor.matmul(h[chunk][:], vw1T_sb[:, kb * P : (kb + 1) * P], q_sb[c][:], start=True, stop=True)
 
         for chunk in range(AHEAD):

@@ -17,7 +17,7 @@ N_PIECES = N // PIECE
 N_BLOCKS = H // P
 N_CHUNKS = N_PIECES * N_BLOCKS
 AHEAD = 4
-WARM_UP = 8
+WARM_UP = 4
 FLOPS = 2 * P * P * N + 2 * 2 * H * P * N
 
 
@@ -26,7 +26,7 @@ def tile_latenthamiltonianpredictor_kernel(tc, table, w, b, q, p, vw1, vb1, vw2,
     with (
         tc.tile_pool(name="held", bufs=1) as held,
         tc.tile_pool(name="work", bufs=3) as work,
-        tc.psum_pool(name="flip", bufs=2) as flip,
+        tc.psum_pool(name="flip", bufs=1) as flip,
         tc.psum_pool(name="hidden", bufs=AHEAD) as hidden,
         tc.psum_pool(name="kicks", bufs=1) as kicks,
     ):
@@ -54,17 +54,17 @@ def tile_latenthamiltonianpredictor_kernel(tc, table, w, b, q, p, vw1, vb1, vw2,
         nc.sync.dma_start(offsets[:], offs)
         nc.sync.dma_start(w_sb[:], w)
         nc.scalar.dma_start(b_sb[:], b)
+        nc.sync.dma_start(p_sb[0][:], p[:, 0:PIECE])
+        nc.scalar.dma_start(p_sb[1][:], p[:, PIECE:N])
 
         identity = held.tile([P, P], BF16)
         make_identity(nc, identity[:])
-        vw1T_sb = held.tile([P, H], BF16)
+        vw1T_ps = flip.tile([P, H], BF16)
         for kb in range(N_BLOCKS):
             block = slice(kb * P, (kb + 1) * P)
-            vw1T_ps = flip.tile([P, P], BF16)
-            nc.tensor.transpose(vw1T_ps[:], vw1_sb[:, block], identity[:])
-            nc.vector.tensor_copy(vw1T_sb[:, block], vw1T_ps[:])
-        for c in range(N_PIECES):
-            nc.gpsimd.dma_start(p_sb[c][:], p[:, c * PIECE : (c + 1) * PIECE])
+            nc.tensor.transpose(vw1T_ps[:, block], vw1_sb[:, block], identity[:])
+        vw1T_sb = held.tile([P, H], BF16)
+        nc.vector.tensor_copy(vw1T_sb[:], vw1T_ps[:])
 
         h = {}
 

@@ -12,10 +12,11 @@ P = 128
 H = 512
 S = 512
 N = 1024
-PIECE = 512
-N_PIECES = N // PIECE
+BANK = 512
 N_BLOCKS = H // P
-N_CHUNKS = N_PIECES * N_BLOCKS
+WIDTHS = (512, 256, 256)
+STARTS = tuple(sum(WIDTHS[:c]) for c in range(len(WIDTHS)))
+CHUNKS = tuple((c, kb) for c in range(len(WIDTHS)) for kb in range(N_BLOCKS))
 AHEAD = 4
 WARM_UP = 4
 FLOPS = 2 * P * P * N + 2 * 2 * H * P * N
@@ -23,19 +24,13 @@ FLOPS = 2 * P * P * N + 2 * 2 * H * P * N
 
 def tile_latenthamiltonianpredictor_kernel(tc, table, w, b, q, p, vw1, vb1, vw2, offs, out):
     nc = tc.nc
+    pieces = range(len(WIDTHS))
     with (
         tc.tile_pool(name="held", bufs=1) as held,
         tc.tile_pool(name="work", bufs=3) as work,
-        tc.psum_pool(name="flip", bufs=1) as flip,
         tc.psum_pool(name="hidden", bufs=AHEAD) as hidden,
         tc.psum_pool(name="kicks", bufs=1) as kicks,
     ):
-        zeros = held.tile([P, PIECE], BF16)
-        nc.vector.memset(zeros[:], 0.0)
-        warm = hidden.tile([P, PIECE], F32, tag="h")
-        for turn in range(WARM_UP):
-            nc.tensor.matmul(warm[:], zeros[:, 0:P], zeros[:], start=True, stop=True)
-
         vw1_sb = held.tile([P, H], BF16)
         vb1_sb = held.tile([P, N_BLOCKS], F32)
         vw2_sb = held.tile([P, N_BLOCKS], F32)
@@ -43,55 +38,62 @@ def tile_latenthamiltonianpredictor_kernel(tc, table, w, b, q, p, vw1, vb1, vw2,
         w_sb = held.tile([P, P], BF16)
         table_sb = held.tile([P, S], BF16)
         b_sb = held.tile([P, 1], F32)
-        q_sb = [held.tile([P, PIECE], BF16, name=f"q_sb{c}") for c in range(N_PIECES)]
-        p_sb = [held.tile([P, PIECE], F32, name=f"p_sb{c}") for c in range(N_PIECES)]
+        q_sb = [held.tile([P, WIDTHS[c]], BF16, name=f"q_sb{c}") for c in pieces]
+        p_sb = [held.tile([P, WIDTHS[c]], F32, name=f"p_sb{c}") for c in pieces]
         nc.sync.dma_start(vw1_sb[:], vw1.rearrange("(r kb) i -> r (kb i)", kb=N_BLOCKS))
-        nc.scalar.dma_start(q_sb[0][:], q[:, 0:PIECE])
         nc.sync.dma_start(vb1_sb[:], vb1.rearrange("(r kb) one -> r (kb one)", kb=N_BLOCKS))
-        nc.scalar.dma_start(q_sb[1][:], q[:, PIECE:N])
         nc.sync.dma_start(vw2_sb[:], vw2.rearrange("(r kb) one -> r (kb one)", kb=N_BLOCKS))
-        nc.scalar.dma_start(table_sb[:], table)
         nc.sync.dma_start(offsets[:], offs)
         nc.sync.dma_start(w_sb[:], w)
+        for c in pieces:
+            nc.scalar.dma_start(q_sb[c][:], q[:, STARTS[c] : STARTS[c] + WIDTHS[c]])
+        nc.scalar.dma_start(table_sb[:], table)
         nc.scalar.dma_start(b_sb[:], b)
-        nc.sync.dma_start(p_sb[0][:], p[:, 0:PIECE])
-        nc.scalar.dma_start(p_sb[1][:], p[:, PIECE:N])
+        for c in pieces:
+            nc.sync.dma_start(p_sb[c][:], p[:, STARTS[c] : STARTS[c] + WIDTHS[c]])
+
+        zeros = held.tile([P, BANK], BF16)
+        nc.vector.memset(zeros[:], 0.0)
+        unused = held.tile([P, 1], F32)
+        nc.scalar.activation(unused[:], zeros[:, 0:1], SIGMOID)
+        warm = hidden.tile([P, BANK], F32, tag="h")
+        for turn in range(WARM_UP):
+            nc.tensor.matmul(warm[:], zeros[:, 0:P], zeros[:], start=True, stop=True)
 
         identity = held.tile([P, P], BF16)
         make_identity(nc, identity[:])
-        vw1T_ps = flip.tile([P, H], BF16)
+        vw1T_sb = held.tile([P, H], BF16)
         for kb in range(N_BLOCKS):
             block = slice(kb * P, (kb + 1) * P)
-            nc.tensor.transpose(vw1T_ps[:, block], vw1_sb[:, block], identity[:])
-        vw1T_sb = held.tile([P, H], BF16)
-        nc.vector.tensor_copy(vw1T_sb[:], vw1T_ps[:])
+            vw1T_ps = hidden.tile([P, P], BF16, tag="h")
+            nc.tensor.transpose(vw1T_ps[:], vw1_sb[:, block], identity[:])
+            nc.vector.tensor_copy(vw1T_sb[:, block], vw1T_ps[:])
 
         h = {}
 
         def hidden_layer(chunk):
-            c, kb = divmod(chunk, N_BLOCKS)
-            h[chunk] = hidden.tile([P, PIECE], F32, name="h", tag="h")
+            c, kb = CHUNKS[chunk]
+            h[chunk] = hidden.tile([P, WIDTHS[c]], F32, name="h", tag="h")
             nc.tensor.matmul(h[chunk][:], vw1T_sb[:, kb * P : (kb + 1) * P], q_sb[c][:], start=True, stop=True)
 
         for chunk in range(AHEAD):
             hidden_layer(chunk)
 
-        kick = [kicks.tile([P, PIECE], F32, name=f"kick{c}") for c in range(N_PIECES)]
-        for c in range(N_PIECES):
-            piece_offsets = offsets[:, c * (PIECE // 16) : (c + 1) * (PIECE // 16)]
+        kick = [kicks.tile([P, WIDTHS[c]], F32, name=f"kick{c}") for c in pieces]
+        for c in pieces:
+            piece_offsets = offsets[:, STARTS[c] // 16 : (STARTS[c] + WIDTHS[c]) // 16]
             nc.tensor.matmul(kick[c][:], w_sb[:], table_sb[:].indirect(piece_offsets), start=True, stop=False)
 
-        for chunk in range(N_CHUNKS):
-            c, kb = divmod(chunk, N_BLOCKS)
-            sig = work.tile([P, PIECE], F32)
+        for chunk, (c, kb) in enumerate(CHUNKS):
+            sig = work.tile([P, WIDTHS[c]], F32)
             nc.scalar.activation(sig[:], h[chunk][:], SIGMOID, bias=vb1_sb[:, kb : kb + 1])
-            if chunk + AHEAD < N_CHUNKS:
+            if chunk + AHEAD < len(CHUNKS):
                 hidden_layer(chunk + AHEAD)
-            minus_s = work.tile([P, PIECE], BF16)
+            minus_s = work.tile([P, WIDTHS[c]], BF16)
             nc.vector.tensor_scalar(minus_s[:], sig[:], vw2_sb[:, kb : kb + 1], -1.0, MULT, MULT)
             last_block = kb == N_BLOCKS - 1
             nc.tensor.matmul(kick[c][:], vw1_sb[:, kb * P : (kb + 1) * P], minus_s[:], start=False, stop=last_block)
             if last_block:
-                result = work.tile([P, PIECE], F32)
+                result = work.tile([P, WIDTHS[c]], F32)
                 nc.vector.scalar_tensor_tensor(result[:], kick[c][:], b_sb[:, 0:1], p_sb[c][:], ADD, ADD)
-                nc.sync.dma_start(out[:, c * PIECE : (c + 1) * PIECE], result[:])
+                nc.sync.dma_start(out[:, STARTS[c] : STARTS[c] + WIDTHS[c]], result[:])

@@ -12,25 +12,30 @@ P = 128
 H = 512
 S = 512
 N = 1024
-BANK = 512
+PIECE = 512
+N_PIECES = N // PIECE
 N_BLOCKS = H // P
-WIDTHS = (512, 256, 256)
-STARTS = tuple(sum(WIDTHS[:c]) for c in range(len(WIDTHS)))
-CHUNKS = tuple((c, kb) for c in range(len(WIDTHS)) for kb in range(N_BLOCKS))
+N_CHUNKS = N_PIECES * N_BLOCKS
 AHEAD = 4
-WARM_UP = 4
+WARM_UP = 8
 FLOPS = 2 * P * P * N + 2 * 2 * H * P * N
 
 
 def tile_latenthamiltonianpredictor_kernel(tc, table, w, b, q, p, vw1, vb1, vw2, offs, out):
     nc = tc.nc
-    pieces = range(len(WIDTHS))
     with (
         tc.tile_pool(name="held", bufs=1) as held,
         tc.tile_pool(name="work", bufs=3) as work,
+        tc.psum_pool(name="flip", bufs=1) as flip,
         tc.psum_pool(name="hidden", bufs=AHEAD) as hidden,
         tc.psum_pool(name="kicks", bufs=1) as kicks,
     ):
+        zeros = held.tile([P, PIECE], BF16)
+        nc.vector.memset(zeros[:], 0.0)
+        warm = hidden.tile([P, PIECE], F32, tag="h")
+        for turn in range(WARM_UP):
+            nc.tensor.matmul(warm[:], zeros[:, 0:P], zeros[:], start=True, stop=True)
+
         vw1_sb = held.tile([P, H], BF16)
         vb1_sb = held.tile([P, N_BLOCKS], F32)
         vw2_sb = held.tile([P, N_BLOCKS], F32)
@@ -38,62 +43,55 @@ def tile_latenthamiltonianpredictor_kernel(tc, table, w, b, q, p, vw1, vb1, vw2,
         w_sb = held.tile([P, P], BF16)
         table_sb = held.tile([P, S], BF16)
         b_sb = held.tile([P, 1], F32)
-        q_sb = [held.tile([P, WIDTHS[c]], BF16, name=f"q_sb{c}") for c in pieces]
-        p_sb = [held.tile([P, WIDTHS[c]], F32, name=f"p_sb{c}") for c in pieces]
+        q_sb = [held.tile([P, PIECE], BF16, name=f"q_sb{c}") for c in range(N_PIECES)]
+        p_sb = [held.tile([P, PIECE], F32, name=f"p_sb{c}") for c in range(N_PIECES)]
         nc.sync.dma_start(vw1_sb[:], vw1.rearrange("(r kb) i -> r (kb i)", kb=N_BLOCKS))
+        nc.scalar.dma_start(q_sb[0][:], q[:, 0:PIECE])
         nc.sync.dma_start(vb1_sb[:], vb1.rearrange("(r kb) one -> r (kb one)", kb=N_BLOCKS))
+        nc.scalar.dma_start(q_sb[1][:], q[:, PIECE:N])
         nc.sync.dma_start(vw2_sb[:], vw2.rearrange("(r kb) one -> r (kb one)", kb=N_BLOCKS))
+        nc.scalar.dma_start(table_sb[:], table)
         nc.sync.dma_start(offsets[:], offs)
         nc.sync.dma_start(w_sb[:], w)
-        for c in pieces:
-            nc.scalar.dma_start(q_sb[c][:], q[:, STARTS[c] : STARTS[c] + WIDTHS[c]])
-        nc.scalar.dma_start(table_sb[:], table)
         nc.scalar.dma_start(b_sb[:], b)
-        for c in pieces:
-            nc.sync.dma_start(p_sb[c][:], p[:, STARTS[c] : STARTS[c] + WIDTHS[c]])
-
-        zeros = held.tile([P, BANK], BF16)
-        nc.vector.memset(zeros[:], 0.0)
-        unused = held.tile([P, 1], F32)
-        nc.scalar.activation(unused[:], zeros[:, 0:1], SIGMOID)
-        warm = hidden.tile([P, BANK], F32, tag="h")
-        for turn in range(WARM_UP):
-            nc.tensor.matmul(warm[:], zeros[:, 0:P], zeros[:], start=True, stop=True)
+        nc.sync.dma_start(p_sb[0][:], p[:, 0:PIECE])
+        nc.scalar.dma_start(p_sb[1][:], p[:, PIECE:N])
 
         identity = held.tile([P, P], BF16)
         make_identity(nc, identity[:])
-        vw1T_sb = held.tile([P, H], BF16)
+        vw1T_ps = flip.tile([P, H], BF16)
         for kb in range(N_BLOCKS):
             block = slice(kb * P, (kb + 1) * P)
-            vw1T_ps = hidden.tile([P, P], BF16, tag="h")
-            nc.tensor.transpose(vw1T_ps[:], vw1_sb[:, block], identity[:])
-            nc.vector.tensor_copy(vw1T_sb[:, block], vw1T_ps[:])
+            nc.tensor.transpose(vw1T_ps[:, block], vw1_sb[:, block], identity[:])
+        vw1T_sb = held.tile([P, H], BF16)
+        nc.vector.tensor_copy(vw1T_sb[:], vw1T_ps[:])
 
         h = {}
 
         def hidden_layer(chunk):
-            c, kb = CHUNKS[chunk]
-            h[chunk] = hidden.tile([P, WIDTHS[c]], F32, name="h", tag="h")
+            c, kb = divmod(chunk, N_BLOCKS)
+            h[chunk] = hidden.tile([P, PIECE], F32, name="h", tag="h")
             nc.tensor.matmul(h[chunk][:], vw1T_sb[:, kb * P : (kb + 1) * P], q_sb[c][:], start=True, stop=True)
 
         for chunk in range(AHEAD):
             hidden_layer(chunk)
 
-        kick = [kicks.tile([P, WIDTHS[c]], F32, name=f"kick{c}") for c in pieces]
-        for c in pieces:
-            piece_offsets = offsets[:, STARTS[c] // 16 : (STARTS[c] + WIDTHS[c]) // 16]
+        kick = [kicks.tile([P, PIECE], F32, name=f"kick{c}") for c in range(N_PIECES)]
+        for c in range(N_PIECES):
+            piece_offsets = offsets[:, c * (PIECE // 16) : (c + 1) * (PIECE // 16)]
             nc.tensor.matmul(kick[c][:], w_sb[:], table_sb[:].indirect(piece_offsets), start=True, stop=False)
 
-        for chunk, (c, kb) in enumerate(CHUNKS):
-            sig = work.tile([P, WIDTHS[c]], F32)
+        for chunk in range(N_CHUNKS):
+            c, kb = divmod(chunk, N_BLOCKS)
+            sig = work.tile([P, PIECE], F32)
             nc.scalar.activation(sig[:], h[chunk][:], SIGMOID, bias=vb1_sb[:, kb : kb + 1])
-            if chunk + AHEAD < len(CHUNKS):
+            if chunk + AHEAD < N_CHUNKS:
                 hidden_layer(chunk + AHEAD)
-            minus_s = work.tile([P, WIDTHS[c]], BF16)
+            minus_s = work.tile([P, PIECE], BF16)
             nc.vector.tensor_scalar(minus_s[:], sig[:], vw2_sb[:, kb : kb + 1], -1.0, MULT, MULT)
             last_block = kb == N_BLOCKS - 1
             nc.tensor.matmul(kick[c][:], vw1_sb[:, kb * P : (kb + 1) * P], minus_s[:], start=False, stop=last_block)
             if last_block:
-                result = work.tile([P, WIDTHS[c]], F32)
+                result = work.tile([P, PIECE], F32)
                 nc.vector.scalar_tensor_tensor(result[:], kick[c][:], b_sb[:, 0:1], p_sb[c][:], ADD, ADD)
-                nc.sync.dma_start(out[:, STARTS[c] : STARTS[c] + WIDTHS[c]], result[:])
+                nc.sync.dma_start(out[:, c * PIECE : (c + 1) * PIECE], result[:])

@@ -26,16 +26,9 @@ def tile_latenthamiltonianpredictor_kernel(tc, table, w, b, q, p, vw1, vb1, vw2,
     with (
         tc.tile_pool(name="held", bufs=1) as held,
         tc.tile_pool(name="work", bufs=3) as work,
-        tc.psum_pool(name="flip", bufs=1) as flip,
         tc.psum_pool(name="hidden", bufs=AHEAD) as hidden,
         tc.psum_pool(name="kicks", bufs=1) as kicks,
     ):
-        zeros = held.tile([P, PIECE], BF16)
-        nc.vector.memset(zeros[:], 0.0)
-        warm = hidden.tile([P, PIECE], F32, tag="h")
-        for turn in range(WARM_UP):
-            nc.tensor.matmul(warm[:], zeros[:, 0:P], zeros[:], start=True, stop=True)
-
         vw1_sb = held.tile([P, H], BF16)
         vb1_sb = held.tile([P, N_BLOCKS], F32)
         vw2_sb = held.tile([P, N_BLOCKS], F32)
@@ -46,25 +39,33 @@ def tile_latenthamiltonianpredictor_kernel(tc, table, w, b, q, p, vw1, vb1, vw2,
         q_sb = [held.tile([P, PIECE], BF16, name=f"q_sb{c}") for c in range(N_PIECES)]
         p_sb = [held.tile([P, PIECE], F32, name=f"p_sb{c}") for c in range(N_PIECES)]
         nc.sync.dma_start(vw1_sb[:], vw1.rearrange("(r kb) i -> r (kb i)", kb=N_BLOCKS))
-        nc.scalar.dma_start(q_sb[0][:], q[:, 0:PIECE])
+        nc.sync.dma_start(q_sb[0][:], q[:, 0:PIECE])
         nc.sync.dma_start(vb1_sb[:], vb1.rearrange("(r kb) one -> r (kb one)", kb=N_BLOCKS))
-        nc.scalar.dma_start(q_sb[1][:], q[:, PIECE:N])
         nc.sync.dma_start(vw2_sb[:], vw2.rearrange("(r kb) one -> r (kb one)", kb=N_BLOCKS))
-        nc.scalar.dma_start(table_sb[:], table)
+        nc.sync.dma_start(table_sb[:], table)
         nc.sync.dma_start(offsets[:], offs)
         nc.sync.dma_start(w_sb[:], w)
-        nc.scalar.dma_start(b_sb[:], b)
-        nc.sync.dma_start(p_sb[0][:], p[:, 0:PIECE])
-        nc.scalar.dma_start(p_sb[1][:], p[:, PIECE:N])
+        nc.sync.dma_start(q_sb[1][:], q[:, PIECE:N])
+        nc.sync.dma_start(b_sb[:], b)
+        for c in range(N_PIECES):
+            nc.sync.dma_start(p_sb[c][:], p[:, c * PIECE : (c + 1) * PIECE])
+
+        zeros = held.tile([P, PIECE], BF16)
+        nc.vector.memset(zeros[:], 0.0)
+        unused = held.tile([P, 1], F32)
+        nc.scalar.activation(unused[:], zeros[:, 0:1], SIGMOID)
+        warm = hidden.tile([P, PIECE], F32, tag="h")
+        for turn in range(WARM_UP):
+            nc.tensor.matmul(warm[:], zeros[:, 0:P], zeros[:], start=True, stop=True)
 
         identity = held.tile([P, P], BF16)
         make_identity(nc, identity[:])
-        vw1T_ps = flip.tile([P, H], BF16)
+        vw1T_sb = held.tile([P, H], BF16)
         for kb in range(N_BLOCKS):
             block = slice(kb * P, (kb + 1) * P)
-            nc.tensor.transpose(vw1T_ps[:, block], vw1_sb[:, block], identity[:])
-        vw1T_sb = held.tile([P, H], BF16)
-        nc.vector.tensor_copy(vw1T_sb[:], vw1T_ps[:])
+            vw1T_ps = hidden.tile([P, P], BF16, tag="h")
+            nc.tensor.transpose(vw1T_ps[:], vw1_sb[:, block], identity[:])
+            nc.vector.tensor_copy(vw1T_sb[:, block], vw1T_ps[:])
 
         h = {}
 

@@ -1,14 +1,15 @@
 import concourse.mybir as mybir
-from concourse.masks import make_identity
 
 BF16 = mybir.dt.bfloat16
 F32 = mybir.dt.float32
 U16 = mybir.dt.uint16
 MULT = mybir.AluOpType.mult
 ADD = mybir.AluOpType.add
+IS_EQUAL = mybir.AluOpType.is_equal
 SIGMOID = mybir.ActivationFunctionType.Sigmoid
 
 P = 128
+SQUARE = 32
 H = 512
 S = 512
 N = 1024
@@ -17,7 +18,7 @@ N_PIECES = N // PIECE
 N_BLOCKS = H // P
 N_CHUNKS = N_PIECES * N_BLOCKS
 AHEAD = 4
-WARM_UP = 8
+WARM_UP = 4
 FLOPS = 2 * P * P * N + 2 * 2 * H * P * N
 
 
@@ -58,8 +59,17 @@ def tile_latenthamiltonianpredictor_kernel(tc, table, w, b, q, p, vw1, vb1, vw2,
         for turn in range(WARM_UP):
             nc.tensor.matmul(warm[:], zeros[:, 0:P], zeros[:], start=True, stop=True)
 
+        ones = held.tile([P, P], F32)
+        nc.vector.memset(ones[:], 1.0)
+        column = held.tile([P, P], F32, align_bytes=64)
+        nc.vector.tensor_tensor_scan(column[:], ones[:], ones[:], -1.0, MULT, ADD)
+        flipped = held.tile([P, P], F32, align_bytes=64)
+        nc.vector.transpose(flipped[:], column[:])
         identity = held.tile([P, P], BF16)
-        make_identity(nc, identity[:])
+        for g in range(P // SQUARE):
+            rows = slice(SQUARE * g, SQUARE * (g + 1))
+            own_row = flipped[rows, SQUARE * g : SQUARE * g + 1]
+            nc.vector.tensor_scalar(identity[rows, :], column[rows, :], own_row, None, IS_EQUAL)
         vw1T_sb = held.tile([P, H], BF16)
         for kb in range(N_BLOCKS):
             block = slice(kb * P, (kb + 1) * P)

@@ -13,12 +13,16 @@ SQUARE = 32
 H = 512
 S = 512
 N = 1024
-PIECE = 512
-N_PIECES = N // PIECE
+BANK = 512
+WIDTHS = [512, 256, 256]
+STARTS = [sum(WIDTHS[:c]) for c in range(len(WIDTHS))]
+N_PIECES = len(WIDTHS)
 N_BLOCKS = H // P
 N_CHUNKS = N_PIECES * N_BLOCKS
 AHEAD = 4
-WARM_UP = 4
+RING = 6
+LAG = 2
+WARM_UP = 2
 FLOPS = 2 * P * P * N + 2 * 2 * H * P * N
 
 
@@ -26,7 +30,7 @@ def tile_latenthamiltonianpredictor_kernel(tc, table, w, b, q, p, vw1, vb1, vw2,
     nc = tc.nc
     with (
         tc.tile_pool(name="held", bufs=1) as held,
-        tc.tile_pool(name="work", bufs=3) as work,
+        tc.tile_pool(name="work", bufs=RING) as work,
         tc.psum_pool(name="hidden", bufs=AHEAD) as hidden,
         tc.psum_pool(name="kicks", bufs=1) as kicks,
     ):
@@ -37,39 +41,45 @@ def tile_latenthamiltonianpredictor_kernel(tc, table, w, b, q, p, vw1, vb1, vw2,
         w_sb = held.tile([P, P], BF16)
         table_sb = held.tile([P, S], BF16)
         b_sb = held.tile([P, 1], F32)
-        q_sb = [held.tile([P, PIECE], BF16, name=f"q_sb{c}") for c in range(N_PIECES)]
-        p_sb = [held.tile([P, PIECE], F32, name=f"p_sb{c}") for c in range(N_PIECES)]
-        nc.sync.dma_start(vw1_sb[:], vw1.rearrange("(r kb) i -> r (kb i)", kb=N_BLOCKS))
-        nc.sync.dma_start(q_sb[0][:], q[:, 0:PIECE])
+        q_sb = [held.tile([P, BANK], BF16, name=f"q_sb{half}") for half in range(N // BANK)]
+        p_sb = [held.tile([P, BANK], F32, name=f"p_sb{half}") for half in range(N // BANK)]
+        vw1_blocks = vw1.rearrange("(r kb) i -> r kb i", kb=N_BLOCKS)
+        nc.sync.dma_start(vw1_sb[:, 0:P], vw1_blocks[:, 0, :])
+        nc.sync.dma_start(q_sb[0][:], q[:, 0:BANK])
         nc.sync.dma_start(vb1_sb[:], vb1.rearrange("(r kb) one -> r (kb one)", kb=N_BLOCKS))
+        nc.sync.dma_start(vw1_sb[:, P:H].rearrange("r (kb i) -> r kb i", i=P), vw1_blocks[:, 1:N_BLOCKS, :])
         nc.sync.dma_start(vw2_sb[:], vw2.rearrange("(r kb) one -> r (kb one)", kb=N_BLOCKS))
         nc.sync.dma_start(table_sb[:], table)
         nc.sync.dma_start(offsets[:], offs)
         nc.sync.dma_start(w_sb[:], w)
-        nc.sync.dma_start(q_sb[1][:], q[:, PIECE:N])
+        nc.sync.dma_start(q_sb[1][:], q[:, BANK:N])
         nc.sync.dma_start(b_sb[:], b)
-        for c in range(N_PIECES):
-            nc.sync.dma_start(p_sb[c][:], p[:, c * PIECE : (c + 1) * PIECE])
+        for half in range(N // BANK):
+            nc.sync.dma_start(p_sb[half][:], p[:, half * BANK : (half + 1) * BANK])
 
-        zeros = held.tile([P, PIECE], BF16)
+        def piece_of(halves, c):
+            half, first = divmod(STARTS[c], BANK)
+            return halves[half][:, first : first + WIDTHS[c]]
+
+        zeros = held.tile([P, BANK], BF16)
         nc.vector.memset(zeros[:], 0.0)
         unused = held.tile([P, 1], F32)
         nc.scalar.activation(unused[:], zeros[:, 0:1], SIGMOID)
-        warm = hidden.tile([P, PIECE], F32, tag="h")
+        warm = hidden.tile([P, BANK], F32, tag="h")
         for turn in range(WARM_UP):
             nc.tensor.matmul(warm[:], zeros[:, 0:P], zeros[:], start=True, stop=True)
 
-        ones = held.tile([P, P], F32)
-        nc.vector.memset(ones[:], 1.0)
-        column = held.tile([P, P], F32, align_bytes=64)
-        nc.vector.tensor_tensor_scan(column[:], ones[:], ones[:], -1.0, MULT, ADD)
-        flipped = held.tile([P, P], F32, align_bytes=64)
-        nc.vector.transpose(flipped[:], column[:])
         identity = held.tile([P, P], BF16)
+        nc.vector.memset(identity[:], 0.0)
+        ones = held.tile([P, SQUARE], F32)
+        nc.vector.memset(ones[:], 1.0)
+        column = held.tile([P, SQUARE], F32, align_bytes=64)
+        nc.vector.tensor_tensor_scan(column[:], ones[:], ones[:], -1.0, MULT, ADD)
+        row = held.tile([P, SQUARE], F32, align_bytes=64)
+        nc.vector.transpose(row[:], column[:])
         for g in range(P // SQUARE):
-            rows = slice(SQUARE * g, SQUARE * (g + 1))
-            own_row = flipped[rows, SQUARE * g : SQUARE * g + 1]
-            nc.vector.tensor_scalar(identity[rows, :], column[rows, :], own_row, None, IS_EQUAL)
+            group = slice(SQUARE * g, SQUARE * (g + 1))
+            nc.vector.tensor_tensor(identity[group, group], column[group, :], row[group, :], IS_EQUAL)
         vw1T_sb = held.tile([P, H], BF16)
         for kb in range(N_BLOCKS):
             block = slice(kb * P, (kb + 1) * P)
@@ -81,28 +91,43 @@ def tile_latenthamiltonianpredictor_kernel(tc, table, w, b, q, p, vw1, vb1, vw2,
 
         def hidden_layer(chunk):
             c, kb = divmod(chunk, N_BLOCKS)
-            h[chunk] = hidden.tile([P, PIECE], F32, name="h", tag="h")
-            nc.tensor.matmul(h[chunk][:], vw1T_sb[:, kb * P : (kb + 1) * P], q_sb[c][:], start=True, stop=True)
+            h[chunk] = hidden.tile([P, WIDTHS[c]], F32, name="h", tag="h")
+            nc.tensor.matmul(h[chunk][:], vw1T_sb[:, kb * P : (kb + 1) * P], piece_of(q_sb, c), start=True, stop=True)
 
         for chunk in range(AHEAD):
             hidden_layer(chunk)
 
-        kick = [kicks.tile([P, PIECE], F32, name=f"kick{c}") for c in range(N_PIECES)]
+        kick = [kicks.tile([P, WIDTHS[c]], F32, name=f"kick{c}") for c in range(N_PIECES)]
         for c in range(N_PIECES):
-            piece_offsets = offsets[:, c * (PIECE // 16) : (c + 1) * (PIECE // 16)]
+            piece_offsets = offsets[:, STARTS[c] // 16 : (STARTS[c] + WIDTHS[c]) // 16]
             nc.tensor.matmul(kick[c][:], w_sb[:], table_sb[:].indirect(piece_offsets), start=True, stop=False)
+        minus_s = {}
 
-        for chunk in range(N_CHUNKS):
+        def sigmoid_and_product(chunk):
             c, kb = divmod(chunk, N_BLOCKS)
-            sig = work.tile([P, PIECE], F32)
+            sig = work.tile([P, WIDTHS[c]], F32, tag="sig")
             nc.scalar.activation(sig[:], h[chunk][:], SIGMOID, bias=vb1_sb[:, kb : kb + 1])
             if chunk + AHEAD < N_CHUNKS:
                 hidden_layer(chunk + AHEAD)
-            minus_s = work.tile([P, PIECE], BF16)
-            nc.vector.tensor_scalar(minus_s[:], sig[:], vw2_sb[:, kb : kb + 1], -1.0, MULT, MULT)
+            minus_s[chunk] = work.tile([P, WIDTHS[c]], BF16, name="minus_s", tag="minus_s")
+            nc.vector.tensor_scalar(minus_s[chunk][:], sig[:], vw2_sb[:, kb : kb + 1], -1.0, MULT, MULT)
+
+        def add_to_kick(chunk):
+            c, kb = divmod(chunk, N_BLOCKS)
             last_block = kb == N_BLOCKS - 1
-            nc.tensor.matmul(kick[c][:], vw1_sb[:, kb * P : (kb + 1) * P], minus_s[:], start=False, stop=last_block)
-            if last_block:
-                result = work.tile([P, PIECE], F32)
-                nc.vector.scalar_tensor_tensor(result[:], kick[c][:], b_sb[:, 0:1], p_sb[c][:], ADD, ADD)
-                nc.sync.dma_start(out[:, c * PIECE : (c + 1) * PIECE], result[:])
+            nc.tensor.matmul(kick[c][:], vw1_sb[:, kb * P : (kb + 1) * P], minus_s[chunk][:], start=False, stop=last_block)
+
+        def finish(chunk):
+            c, kb = divmod(chunk, N_BLOCKS)
+            if kb == N_BLOCKS - 1:
+                result = work.tile([P, WIDTHS[c]], F32, tag="result")
+                nc.vector.scalar_tensor_tensor(result[:], kick[c][:], b_sb[:, 0:1], piece_of(p_sb, c), ADD, ADD)
+                nc.sync.dma_start(out[:, STARTS[c] : STARTS[c] + WIDTHS[c]], result[:])
+
+        for step in range(N_CHUNKS + LAG + 1):
+            if step < N_CHUNKS:
+                sigmoid_and_product(step)
+            if 0 <= step - LAG < N_CHUNKS:
+                add_to_kick(step - LAG)
+            if 0 <= step - LAG - 1:
+                finish(step - LAG - 1)

@@ -22,7 +22,7 @@ N_CHUNKS = N_PIECES * N_BLOCKS
 AHEAD = 4
 RING = 6
 LAG = 2
-WARM_UP = 2
+WARM_UP = 12
 FLOPS = 2 * P * P * N + 2 * 2 * H * P * N
 
 
@@ -61,13 +61,13 @@ def tile_latenthamiltonianpredictor_kernel(tc, table, w, b, q, p, vw1, vb1, vw2,
             half, first = divmod(STARTS[c], BANK)
             return halves[half][:, first : first + WIDTHS[c]]
 
-        zeros = held.tile([P, BANK], BF16)
+        zeros = held.tile([P, P], BF16)
         nc.vector.memset(zeros[:], 0.0)
         unused = held.tile([P, 1], F32)
         nc.scalar.activation(unused[:], zeros[:, 0:1], SIGMOID)
-        warm = hidden.tile([P, BANK], F32, tag="h")
+        warm = hidden.tile([P, P], F32, tag="h")
         for turn in range(WARM_UP):
-            nc.tensor.matmul(warm[:], zeros[:, 0:P], zeros[:], start=True, stop=True)
+            nc.tensor.matmul(warm[:], zeros[:], zeros[:], start=True, stop=True)
 
         identity = held.tile([P, P], BF16)
         nc.vector.memset(identity[:], 0.0)

@@ -14,7 +14,7 @@ H = 512
 S = 512
 N = 1024
 BANK = 512
-WIDTHS = [512, 256, 256]
+WIDTHS = [512, 320, 192]
 STARTS = [sum(WIDTHS[:c]) for c in range(len(WIDTHS))]
 N_PIECES = len(WIDTHS)
 N_BLOCKS = H // P
@@ -45,9 +45,9 @@ def tile_latenthamiltonianpredictor_kernel(tc, table, w, b, q, p, vw1, vb1, vw2,
         p_sb = [held.tile([P, BANK], F32, name=f"p_sb{half}") for half in range(N // BANK)]
         vw1_blocks = vw1.rearrange("(r kb) i -> r kb i", kb=N_BLOCKS)
         nc.sync.dma_start(vw1_sb[:, 0:P], vw1_blocks[:, 0, :])
+        nc.sync.dma_start(vw1_sb[:, P:H].rearrange("r (kb i) -> r kb i", i=P), vw1_blocks[:, 1:N_BLOCKS, :])
         nc.sync.dma_start(q_sb[0][:], q[:, 0:BANK])
         nc.sync.dma_start(vb1_sb[:], vb1.rearrange("(r kb) one -> r (kb one)", kb=N_BLOCKS))
-        nc.sync.dma_start(vw1_sb[:, P:H].rearrange("r (kb i) -> r kb i", i=P), vw1_blocks[:, 1:N_BLOCKS, :])
         nc.sync.dma_start(vw2_sb[:], vw2.rearrange("(r kb) one -> r (kb one)", kb=N_BLOCKS))
         nc.sync.dma_start(table_sb[:], table)
         nc.sync.dma_start(offsets[:], offs)

@@ -21,7 +21,7 @@ N_BLOCKS = H // P
 N_CHUNKS = N_PIECES * N_BLOCKS
 AHEAD = 4
 RING = 6
-LAG = 2
+LAG = 1
 WARM_UP = 12
 FLOPS = 2 * P * P * N + 2 * 2 * H * P * N
 

@@ -110,7 +110,8 @@ def tile_latenthamiltonianpredictor_kernel(tc, table, w, b, q, p, vw1, vb1, vw2,
             if chunk + AHEAD < N_CHUNKS:
                 hidden_layer(chunk + AHEAD)
             minus_s[chunk] = work.tile([P, WIDTHS[c]], BF16, name="minus_s", tag="minus_s")
-            nc.vector.tensor_scalar(minus_s[chunk][:], sig[:], vw2_sb[:, kb : kb + 1], -1.0, MULT, MULT)
+            engine = nc.gpsimd if c == 1 and kb % 2 == 0 else nc.vector
+            engine.tensor_scalar(minus_s[chunk][:], sig[:], vw2_sb[:, kb : kb + 1], -1.0, MULT, MULT)
 
         def add_to_kick(chunk):
             c, kb = divmod(chunk, N_BLOCKS)

@@ -47,11 +47,11 @@ def tile_latenthamiltonianpredictor_kernel(tc, table, w, b, q, p, vw1, vb1, vw2,
         nc.sync.dma_start(vw1_sb[:, 0:P], vw1_blocks[:, 0, :])
         nc.sync.dma_start(vw1_sb[:, P:H].rearrange("r (kb i) -> r kb i", i=P), vw1_blocks[:, 1:N_BLOCKS, :])
         nc.sync.dma_start(q_sb[0][:], q[:, 0:BANK])
-        nc.sync.dma_start(vb1_sb[:], vb1.rearrange("(r kb) one -> r (kb one)", kb=N_BLOCKS))
-        nc.sync.dma_start(vw2_sb[:], vw2.rearrange("(r kb) one -> r (kb one)", kb=N_BLOCKS))
         nc.sync.dma_start(table_sb[:], table)
         nc.sync.dma_start(offsets[:], offs)
         nc.sync.dma_start(w_sb[:], w)
+        nc.sync.dma_start(vb1_sb[:], vb1.rearrange("(r kb) one -> r (kb one)", kb=N_BLOCKS))
+        nc.sync.dma_start(vw2_sb[:], vw2.rearrange("(r kb) one -> r (kb one)", kb=N_BLOCKS))
         nc.sync.dma_start(q_sb[1][:], q[:, BANK:N])
         nc.sync.dma_start(b_sb[:], b)
         for half in range(N // BANK):

@@ -45,8 +45,9 @@ def tile_latenthamiltonianpredictor_kernel(tc, table, w, b, q, p, vw1, vb1, vw2,
         p_sb = [held.tile([P, BANK], F32, name=f"p_sb{half}") for half in range(N // BANK)]
         vw1_blocks = vw1.rearrange("(r kb) i -> r kb i", kb=N_BLOCKS)
         nc.sync.dma_start(vw1_sb[:, 0:P], vw1_blocks[:, 0, :])
-        nc.sync.dma_start(vw1_sb[:, P:H].rearrange("r (kb i) -> r kb i", i=P), vw1_blocks[:, 1:N_BLOCKS, :])
+        nc.sync.dma_start(vw1_sb[:, P : 2 * P], vw1_blocks[:, 1, :])
         nc.sync.dma_start(q_sb[0][:], q[:, 0:BANK])
+        nc.sync.dma_start(vw1_sb[:, 2 * P : H].rearrange("r (kb i) -> r kb i", i=P), vw1_blocks[:, 2:N_BLOCKS, :])
         nc.sync.dma_start(table_sb[:], table)
         nc.sync.dma_start(offsets[:], offs)
         nc.sync.dma_start(w_sb[:], w)

@@ -46,8 +46,8 @@ def tile_latenthamiltonianpredictor_kernel(tc, table, w, b, q, p, vw1, vb1, vw2,
         vw1_blocks = vw1.rearrange("(r kb) i -> r kb i", kb=N_BLOCKS)
         nc.sync.dma_start(vw1_sb[:, 0:P], vw1_blocks[:, 0, :])
         nc.sync.dma_start(vw1_sb[:, P : 2 * P], vw1_blocks[:, 1, :])
-        nc.sync.dma_start(q_sb[0][:], q[:, 0:BANK])
         nc.sync.dma_start(vw1_sb[:, 2 * P : H].rearrange("r (kb i) -> r kb i", i=P), vw1_blocks[:, 2:N_BLOCKS, :])
+        nc.sync.dma_start(q_sb[0][:], q[:, 0:BANK])
         nc.sync.dma_start(table_sb[:], table)
         nc.sync.dma_start(offsets[:], offs)
         nc.sync.dma_start(w_sb[:], w)

@@ -17,6 +17,8 @@ BANK = 512
 WIDTHS = [512, 320, 192]
 STARTS = [sum(WIDTHS[:c]) for c in range(len(WIDTHS))]
 N_PIECES = len(WIDTHS)
+STORE_WIDTHS = [512, 256, 256]
+STORE_STARTS = [sum(STORE_WIDTHS[:c]) for c in range(N_PIECES)]
 N_BLOCKS = H // P
 N_CHUNKS = N_PIECES * N_BLOCKS
 AHEAD = 4
@@ -103,6 +105,7 @@ def tile_latenthamiltonianpredictor_kernel(tc, table, w, b, q, p, vw1, vb1, vw2,
             piece_offsets = offsets[:, STARTS[c] // 16 : (STARTS[c] + WIDTHS[c]) // 16]
             nc.tensor.matmul(kick[c][:], w_sb[:], table_sb[:].indirect(piece_offsets), start=True, stop=False)
         minus_s = {}
+        result = held.tile([P, N], F32)
 
         def sigmoid_and_product(chunk):
             c, kb = divmod(chunk, N_BLOCKS)
@@ -122,9 +125,10 @@ def tile_latenthamiltonianpredictor_kernel(tc, table, w, b, q, p, vw1, vb1, vw2,
         def finish(chunk):
             c, kb = divmod(chunk, N_BLOCKS)
             if kb == N_BLOCKS - 1:
-                result = work.tile([P, WIDTHS[c]], F32, tag="result")
-                nc.vector.scalar_tensor_tensor(result[:], kick[c][:], b_sb[:, 0:1], piece_of(p_sb, c), ADD, ADD)
-                nc.sync.dma_start(out[:, STARTS[c] : STARTS[c] + WIDTHS[c]], result[:])
+                summed = slice(STARTS[c], STARTS[c] + WIDTHS[c])
+                nc.vector.scalar_tensor_tensor(result[:, summed], kick[c][:], b_sb[:, 0:1], piece_of(p_sb, c), ADD, ADD)
+                stored = slice(STORE_STARTS[c], STORE_STARTS[c] + STORE_WIDTHS[c])
+                nc.sync.dma_start(out[:, stored], result[:, stored])
 
         for step in range(N_CHUNKS + LAG + 1):
             if step < N_CHUNKS:

import concourse.mybir as mybir

BF16 = mybir.dt.bfloat16
F32 = mybir.dt.float32
U16 = mybir.dt.uint16
MULT = mybir.AluOpType.mult
ADD = mybir.AluOpType.add
IS_EQUAL = mybir.AluOpType.is_equal
SIGMOID = mybir.ActivationFunctionType.Sigmoid

P = 128
SQUARE = 32
H = 512
S = 512
N = 1024
BANK = 512
WIDTHS = [512, 320, 192]
STARTS = [sum(WIDTHS[:c]) for c in range(len(WIDTHS))]
N_PIECES = len(WIDTHS)
STORE_WIDTHS = [512, 256, 256]
STORE_STARTS = [sum(STORE_WIDTHS[:c]) for c in range(N_PIECES)]
N_BLOCKS = H // P
N_CHUNKS = N_PIECES * N_BLOCKS
AHEAD = 4
RING = 6
LAG = 1
WARM_UP = 12
FLOPS = 2 * P * P * N + 2 * 2 * H * P * N


def tile_latenthamiltonianpredictor_kernel(tc, table, w, b, q, p, vw1, vb1, vw2, offs, out):
    nc = tc.nc
    with (
        tc.tile_pool(name="held", bufs=1) as held,
        tc.tile_pool(name="work", bufs=RING) as work,
        tc.psum_pool(name="hidden", bufs=AHEAD) as hidden,
        tc.psum_pool(name="kicks", bufs=1) as kicks,
    ):
        vw1_sb = held.tile([P, H], BF16)
        vb1_sb = held.tile([P, N_BLOCKS], F32)
        vw2_sb = held.tile([P, N_BLOCKS], F32)
        offsets = held.tile([P, N // 16], U16)
        w_sb = held.tile([P, P], BF16)
        table_sb = held.tile([P, S], BF16)
        b_sb = held.tile([P, 1], F32)
        q_sb = [held.tile([P, BANK], BF16, name=f"q_sb{half}") for half in range(N // BANK)]
        p_sb = [held.tile([P, BANK], F32, name=f"p_sb{half}") for half in range(N // BANK)]
        vw1_blocks = vw1.rearrange("(r kb) i -> r kb i", kb=N_BLOCKS)
        nc.sync.dma_start(vw1_sb[:, 0:P], vw1_blocks[:, 0, :])
        nc.sync.dma_start(vw1_sb[:, P : 2 * P], vw1_blocks[:, 1, :])
        nc.sync.dma_start(vw1_sb[:, 2 * P : H].rearrange("r (kb i) -> r kb i", i=P), vw1_blocks[:, 2:N_BLOCKS, :])
        nc.sync.dma_start(q_sb[0][:], q[:, 0:BANK])
        nc.sync.dma_start(table_sb[:], table)
        nc.sync.dma_start(offsets[:], offs)
        nc.sync.dma_start(w_sb[:], w)
        nc.sync.dma_start(vb1_sb[:], vb1.rearrange("(r kb) one -> r (kb one)", kb=N_BLOCKS))
        nc.sync.dma_start(vw2_sb[:], vw2.rearrange("(r kb) one -> r (kb one)", kb=N_BLOCKS))
        nc.sync.dma_start(q_sb[1][:], q[:, BANK:N])
        nc.sync.dma_start(b_sb[:], b)
        for half in range(N // BANK):
            nc.sync.dma_start(p_sb[half][:], p[:, half * BANK : (half + 1) * BANK])

        def piece_of(halves, c):
            half, first = divmod(STARTS[c], BANK)
            return halves[half][:, first : first + WIDTHS[c]]

        zeros = held.tile([P, P], BF16)
        nc.vector.memset(zeros[:], 0.0)
        unused = held.tile([P, 1], F32)
        nc.scalar.activation(unused[:], zeros[:, 0:1], SIGMOID)
        warm = hidden.tile([P, P], F32, tag="h")
        for turn in range(WARM_UP):
            nc.tensor.matmul(warm[:], zeros[:], zeros[:], start=True, stop=True)

        identity = held.tile([P, P], BF16)
        nc.vector.memset(identity[:], 0.0)
        ones = held.tile([P, SQUARE], F32)
        nc.vector.memset(ones[:], 1.0)
        column = held.tile([P, SQUARE], F32, align_bytes=64)
        nc.vector.tensor_tensor_scan(column[:], ones[:], ones[:], -1.0, MULT, ADD)
        row = held.tile([P, SQUARE], F32, align_bytes=64)
        nc.vector.transpose(row[:], column[:])
        for g in range(P // SQUARE):
            group = slice(SQUARE * g, SQUARE * (g + 1))
            nc.vector.tensor_tensor(identity[group, group], column[group, :], row[group, :], IS_EQUAL)
        vw1T_sb = held.tile([P, H], BF16)
        for kb in range(N_BLOCKS):
            block = slice(kb * P, (kb + 1) * P)
            vw1T_ps = hidden.tile([P, P], BF16, tag="h")
            nc.tensor.transpose(vw1T_ps[:], vw1_sb[:, block], identity[:])
            nc.vector.tensor_copy(vw1T_sb[:, block], vw1T_ps[:])

        h = {}

        def hidden_layer(chunk):
            c, kb = divmod(chunk, N_BLOCKS)
            h[chunk] = hidden.tile([P, WIDTHS[c]], F32, name="h", tag="h")
            nc.tensor.matmul(h[chunk][:], vw1T_sb[:, kb * P : (kb + 1) * P], piece_of(q_sb, c), start=True, stop=True)

        for chunk in range(AHEAD):
            hidden_layer(chunk)

        kick = [kicks.tile([P, WIDTHS[c]], F32, name=f"kick{c}") for c in range(N_PIECES)]
        for c in range(N_PIECES):
            piece_offsets = offsets[:, STARTS[c] // 16 : (STARTS[c] + WIDTHS[c]) // 16]
            nc.tensor.matmul(kick[c][:], w_sb[:], table_sb[:].indirect(piece_offsets), start=True, stop=False)
        minus_s = {}
        result = held.tile([P, N], F32)

        def sigmoid_and_product(chunk):
            c, kb = divmod(chunk, N_BLOCKS)
            sig = work.tile([P, WIDTHS[c]], F32, tag="sig")
            nc.scalar.activation(sig[:], h[chunk][:], SIGMOID, bias=vb1_sb[:, kb : kb + 1])
            if chunk + AHEAD < N_CHUNKS:
                hidden_layer(chunk + AHEAD)
            minus_s[chunk] = work.tile([P, WIDTHS[c]], BF16, name="minus_s", tag="minus_s")
            engine = nc.gpsimd if c == 1 and kb % 2 == 0 else nc.vector
            engine.tensor_scalar(minus_s[chunk][:], sig[:], vw2_sb[:, kb : kb + 1], -1.0, MULT, MULT)

        def add_to_kick(chunk):
            c, kb = divmod(chunk, N_BLOCKS)
            last_block = kb == N_BLOCKS - 1
            nc.tensor.matmul(kick[c][:], vw1_sb[:, kb * P : (kb + 1) * P], minus_s[chunk][:], start=False, stop=last_block)

        def finish(chunk):
            c, kb = divmod(chunk, N_BLOCKS)
            if kb == N_BLOCKS - 1:
                summed = slice(STARTS[c], STARTS[c] + WIDTHS[c])
                nc.vector.scalar_tensor_tensor(result[:, summed], kick[c][:], b_sb[:, 0:1], piece_of(p_sb, c), ADD, ADD)
                stored = slice(STORE_STARTS[c], STORE_STARTS[c] + STORE_WIDTHS[c])
                nc.sync.dma_start(out[:, stored], result[:, stored])

        for step in range(N_CHUNKS + LAG + 1):
            if step < N_CHUNKS:
                sigmoid_and_product(step)
            if 0 <= step - LAG < N_CHUNKS:
                add_to_kick(step - LAG)
            if 0 <= step - LAG - 1:
                finish(step - LAG - 1)
